import numpy as np
import ml_dtypes


def mxq(x, axis, fmt="e4m3"):
    dtype, down = {"e4m3": (ml_dtypes.float8_e4m3fn, 7), "e5m2": (ml_dtypes.float8_e5m2, 14)}[fmt]
    v = np.moveaxis(np.asarray(x, np.float32).astype(ml_dtypes.bfloat16).astype(np.float64), axis, -1)
    blocks = v.reshape(v.shape[:-1] + (-1, 32))
    amax = np.abs(blocks).max(-1, keepdims=True)
    byte = np.maximum(np.where(amax > 0, np.frexp(amax)[1] - 1 + 127, 0) - down, 1)
    scale = np.exp2(byte - 127.0)
    codes = (blocks / scale).astype(np.float32).astype(dtype).astype(np.float64)
    return np.moveaxis((codes * scale).reshape(v.shape), -1, axis)


WIDE = False


def mx_kscale(k):
    if not WIDE:
        return np.ones(k)
    levels = np.array([10, -10, 5, -5, 0])
    a = np.random.permutation(np.resize(levels, k // 512 * 4)).reshape(k // 512, 4)
    idx = np.arange(k)
    return np.exp2(a[idx // 512, idx % 128 // 32])


BF16 = ml_dtypes.bfloat16


def bf(x):
    return np.asarray(x, np.float32).astype(BF16)


def f64(x):
    return np.asarray(x).astype(np.float64)


E2M1 = np.array([0.0, 0.5, 1.0, 1.5, 2.0, 3.0, 4.0, 6.0, -0.0, -0.5, -1.0, -1.5, -2.0, -3.0, -4.0, -6.0])


def pack_weight(w, fmt):
    k, n = w.shape
    w = f64(bf(w)).reshape(k // 32, 32, n)
    amax = np.abs(w).max(1)
    if fmt == "e4m3":
        byte = np.frexp(amax)[1] - 1 + 127 - 7
    else:
        mant, ex = np.frexp(amax / 6.0)
        byte = np.where(mant > 0.5, ex, ex - 1) + 127
    byte = np.clip(np.where(amax > 0, byte, 1), 1, 254)
    scaled = (w * np.exp2(127.0 - byte)[:, None, :]).reshape(k, n).astype(np.float32)
    by_word = np.ascontiguousarray(scaled.reshape(k // 512, 128, 4, n).transpose(0, 1, 3, 2))
    if fmt == "e4m3":
        words = by_word.astype(ml_dtypes.float8_e4m3fn).view(np.uint8)
    else:
        c = by_word.astype(ml_dtypes.float4_e2m1fn).view(np.uint8) & 0xF
        words = c[..., 0::2] | (c[..., 1::2] << 4)
    return np.ascontiguousarray(words), np.ascontiguousarray(byte.astype(np.uint8).reshape(k // 512, 16, n))


def unpack_weight(words, scales, fmt):
    g, p, n, _ = words.shape
    if fmt == "e4m3":
        vals = np.ascontiguousarray(words).view(ml_dtypes.float8_e4m3fn).astype(np.float64)
    else:
        nib = np.empty((g, p, n, 4), np.uint8)
        nib[..., 0::2] = words & 0xF
        nib[..., 1::2] = words >> 4
        vals = E2M1[nib]
    vals = vals * np.repeat(np.exp2(scales.astype(np.float64) - 127.0), 8, axis=1)[..., None]
    return vals.transpose(0, 1, 3, 2).reshape(g * 512, n)

def pack4(w):
    words, scales = pack_weight(w, "e2m1")
    return words.reshape(words.shape[0], 128, -1), scales


def unpack4(words, scales):
    return unpack_weight(words.reshape(words.shape[0], 128, -1, 2), scales, "e2m1")


B, S, D = 1, 512, 2048
ROPE_BASE = 10000.0


def rope_tables():
    inv_freq = 1.0 / ROPE_BASE ** (np.arange(0, D, 2) / D)
    freqs = np.outer(np.arange(S), inv_freq)
    emb = np.concatenate([freqs, freqs], axis=-1)
    return np.cos(emb), np.sin(emb)


def rotate_half(u):
    u1, u2 = np.split(u, 2, axis=-1)
    return np.concatenate([-u2, u1], axis=-1)


def setup_inputs():
    s = mx_kscale(D)
    c, sn = rope_tables()
    w = 1.0 / np.sqrt(D)
    x = bf(np.random.standard_normal((B, S, D)) * s)
    wq = np.random.standard_normal((D, D)) * w / s[None, :]
    wk = np.random.standard_normal((D, D)) * w / s[None, :]
    wq_words, wq_scales = pack4(np.ascontiguousarray(wq.T))
    wk_words, wk_scales = pack4(np.ascontiguousarray(wk.T))
    return {"x": x,
            "cos": bf(c),
            "sin": bf(sn),
            "Wq_words": wq_words,
            "Wq_scales": wq_scales,
            "Wk_words": wk_words,
            "Wk_scales": wk_scales}


def reference(x, cos, sin, Wq_words, Wq_scales, Wk_words, Wk_scales):
    xq = mxq(f64(x), 2, "e4m3")
    q = xq @ unpack4(Wq_words, Wq_scales)
    k = xq @ unpack4(Wk_words, Wk_scales)
    c, sn = f64(cos), f64(sin)
    q_rot = q * c + rotate_half(q) * sn
    k_rot = k * c + rotate_half(k) * sn
    return q_rot, k_rot

@@ -1,0 +1,175 @@
+from contextlib import ExitStack
+
+import concourse.mybir as mybir
+from concourse.masks import make_identity
+
+F32 = mybir.dt.float32
+BF16 = mybir.dt.bfloat16
+I32 = mybir.dt.int32
+U32 = mybir.dt.uint32
+U8 = mybir.dt.uint8
+FP8X4 = mybir.dt.float8_e4m3fn_x4
+FP4X4 = mybir.dt.float4_e2m1fn_x4
+MULT = mybir.AluOpType.mult
+ADD = mybir.AluOpType.add
+
+P = 128
+TOKENS = 512
+K = 2048
+N = 2048
+HALF = N // 2
+PACK = 4
+K_PASS = P * PACK
+K_GROUPS = K // K_PASS
+TOKEN_TILES = TOKENS // P
+BANK = 512
+PAIRS = HALF // BANK
+PSUM_BANKS = 8
+WORDS_PER_GROUP = K_PASS // 2
+SCALE_ROWS = K_PASS // 32
+
+FLOPS = 2 * 2 * TOKENS * K * N
+
+
+def load_weight(nc, words_dram, scales_dram, words, plane):
+    for g in range(0, K_GROUPS, 2):
+        for s in range(SCALE_ROWS // 2):
+            first = 32 * (s // 4) + s % 4
+            nc.sync.dma_start(
+                out=plane[first : P : P // 2, g : g + 2, :].bitcast(I32),
+                in_=scales_dram[g : g + 2, s : SCALE_ROWS : SCALE_ROWS // 2, :]
+                .bitcast(I32)
+                .rearrange("g s n -> s g n"),
+            )
+    for g in range(K_GROUPS):
+        nc.sync.dma_start(out=words[g][:].bitcast(I32), in_=words_dram[g].bitcast(I32))
+
+
+def transpose_tokens(nc, psum, x_tile, ident, grouped):
+    x_words = x_tile[:].bitcast(F32)
+    grouped_words = grouped[:].bitcast(F32).rearrange("p (g r u) -> p g r u", g=K_GROUPS, u=2)
+    for g in range(0, K_GROUPS, 2):
+        turned = psum.tile([P, 2, 2, P], F32, tag="bank")
+        for i in range(2):
+            for u in range(2):
+                start = (g + i) * WORDS_PER_GROUP + u
+                nc.tensor.transpose(
+                    turned[:, i, u, :],
+                    x_words[:, start : (g + i + 1) * WORDS_PER_GROUP : 2],
+                    ident[:],
+                )
+        nc.scalar.copy(
+            out=grouped_words[:, g : g + 2, :, :],
+            in_=turned[:].rearrange("p g u r -> p g r u"),
+        )
+
+
+def tile_attention_pa_kernel(
+    tc, x, cos, sin, Wq_words, Wq_scales, Wk_words, Wk_scales, out_0, out_1
+):
+    nc = tc.nc
+    x_rows = x.flatten_outer_dims()
+    outs_dram = (out_0.flatten_outer_dims(), out_1.flatten_outer_dims())
+
+    with ExitStack() as ctx:
+        ctx.enter_context(tc.manual_schedule())
+        keep = ctx.enter_context(tc.tile_pool(name="keep", bufs=1))
+        parts = ctx.enter_context(tc.tile_pool(name="parts", bufs=3))
+        results = ctx.enter_context(tc.tile_pool(name="results", bufs=4))
+        psum = ctx.enter_context(tc.psum_pool(name="psum", bufs=PSUM_BANKS))
+
+        ident = keep.tile([P, P], F32, name="ident")
+        x_sb = [keep.tile([P, K], BF16, name="x%d" % m) for m in range(TOKEN_TILES)]
+        cos_sb = [keep.tile([P, N], BF16, name="cos%d" % m) for m in range(TOKEN_TILES)]
+        sin_sb = [keep.tile([P, N], BF16, name="sin%d" % m) for m in range(TOKEN_TILES)]
+        grouped = [
+            keep.tile([P, K], BF16, name="grouped%d" % m, align_bytes=64)
+            for m in range(TOKEN_TILES)
+        ]
+        x_codes = [
+            keep.tile([P, K // PACK], U32, name="x_codes%d" % m, align_bytes=64)
+            for m in range(TOKEN_TILES)
+        ]
+        x_scales = [
+            keep.tile([P, K // PACK], U8, name="x_scales%d" % m, align_bytes=64)
+            for m in range(TOKEN_TILES)
+        ]
+        w_words = [
+            [
+                keep.tile([P, 2 * N], U8, name="w_words%d_%d" % (w, g), align_bytes=64)
+                for g in range(K_GROUPS)
+            ]
+            for w in range(2)
+        ]
+        w_planes = [
+            keep.tile([P, K_GROUPS, N], U8, name="w_plane%d" % w, align_bytes=64)
+            for w in range(2)
+        ]
+
+        make_identity(nc, ident[:])
+        for w in range(2):
+            nc.vector.memset(w_planes[w][:].bitcast(I32), 0)
+
+        for m in range(TOKEN_TILES):
+            nc.sync.dma_start(out=x_sb[m][:], in_=x_rows[m * P : (m + 1) * P, :])
+        load_weight(nc, Wq_words, Wq_scales, w_words[0], w_planes[0])
+        for m in range(TOKEN_TILES):
+            nc.sync.dma_start(out=cos_sb[m][:], in_=cos[m * P : (m + 1) * P, :])
+            nc.sync.dma_start(out=sin_sb[m][:], in_=sin[m * P : (m + 1) * P, :])
+        load_weight(nc, Wk_words, Wk_scales, w_words[1], w_planes[1])
+
+        for m in range(TOKEN_TILES):
+            transpose_tokens(nc, psum, x_sb[m], ident, grouped[m])
+        for m in range(TOKEN_TILES):
+            nc.vector.quantize_mx(
+                out=x_codes[m][:].bitcast(FP8X4), scales=x_scales[m][:], in_=grouped[m][:]
+            )
+
+        for w in range(2):
+            for m in range(TOKEN_TILES):
+                rotated = results.tile([P, 2, PAIRS, BANK], F32)
+                for j in range(PAIRS):
+                    low_start = j * BANK
+                    high_start = HALF + j * BANK
+                    low = slice(low_start, low_start + BANK)
+                    high = slice(high_start, high_start + BANK)
+                    acc_low = psum.tile([P, BANK], F32, tag="bank")
+                    acc_high = psum.tile([P, BANK], F32, tag="bank")
+                    for g in range(K_GROUPS):
+                        tokens = slice(g * P, (g + 1) * P)
+                        for acc, first in ((acc_low, low_start), (acc_high, high_start)):
+                            nc.tensor.matmul_mx(
+                                out=acc[:],
+                                lhsT=x_codes[m][:, tokens].bitcast(FP8X4),
+                                lhsT_scale=x_scales[m][:, tokens],
+                                rhs=w_words[w][g][:, 2 * first : 2 * (first + BANK)].bitcast(FP4X4),
+                                rhs_scale=w_planes[w][:, g, first : first + BANK],
+                                start=(g == 0),
+                                stop=(g == K_GROUPS - 1),
+                            )
+                    by_cos = parts.tile([P, 2, BANK], F32)
+                    by_sin = parts.tile([P, 2, BANK], F32)
+                    nc.vector.tensor_tensor(
+                        out=by_cos[:, 0, :], in0=acc_low[:], in1=cos_sb[m][:, low], op=MULT
+                    )
+                    nc.vector.tensor_tensor(
+                        out=by_sin[:, 1, :], in0=acc_low[:], in1=sin_sb[m][:, high], op=MULT
+                    )
+                    nc.vector.tensor_tensor(
+                        out=by_cos[:, 1, :], in0=acc_high[:], in1=cos_sb[m][:, high], op=MULT
+                    )
+                    nc.vector.scalar_tensor_tensor(
+                        out=by_sin[:, 0, :],
+                        in0=acc_high[:],
+                        scalar=-1.0,
+                        in1=sin_sb[m][:, low],
+                        op0=MULT,
+                        op1=MULT,
+                    )
+                    nc.gpsimd.tensor_tensor(
+                        out=rotated[:, :, j, :], in0=by_cos[:], in1=by_sin[:], op=ADD
+                    )
+                nc.sync.dma_start(
+                    out=outs_dram[w][m * P : (m + 1) * P, :],
+                    in_=rotated[:].rearrange("p h j c -> p (h j c)"),
+                )

@@ -24,14 +24,22 @@ K_GROUPS = K // K_PASS
 TOKEN_TILES = TOKENS // P
 BANK = 512
 PAIRS = HALF // BANK
+LOW = 0
+HIGH = 1
 PSUM_BANKS = 8
 WORDS_PER_GROUP = K_PASS // 2
 SCALE_ROWS = K_PASS // 32
+FP4_WORD_BYTES = 2
 
 FLOPS = 2 * 2 * TOKENS * K * N
 
 
-def load_weight(nc, words_dram, scales_dram, words, plane):
+def pair_columns(rows, j):
+    width = rows.shape[1] // (2 * PAIRS)
+    return rows.rearrange("r (h c) -> r h c", h=2)[:, :, j * width : (j + 1) * width]
+
+
+def load_scales(nc, scales_dram, plane):
     for g in range(0, K_GROUPS, 2):
         for s in range(SCALE_ROWS // 2):
             first = 32 * (s // 4) + s % 4
@@ -41,8 +49,6 @@ def load_weight(nc, words_dram, scales_dram, words, plane):
                 .bitcast(I32)
                 .rearrange("g s n -> s g n"),
             )
-    for g in range(K_GROUPS):
-        nc.sync.dma_start(out=words[g][:].bitcast(I32), in_=words_dram[g].bitcast(I32))
 
 
 def transpose_tokens(nc, psum, x_tile, ident, grouped):
@@ -69,19 +75,19 @@ def tile_attention_pa_kernel(
 ):
     nc = tc.nc
     x_rows = x.flatten_outer_dims()
+    words_dram = (Wq_words, Wk_words)
+    scales_dram = (Wq_scales, Wk_scales)
     outs_dram = (out_0.flatten_outer_dims(), out_1.flatten_outer_dims())
 
     with ExitStack() as ctx:
         ctx.enter_context(tc.manual_schedule())
         keep = ctx.enter_context(tc.tile_pool(name="keep", bufs=1))
         parts = ctx.enter_context(tc.tile_pool(name="parts", bufs=3))
-        results = ctx.enter_context(tc.tile_pool(name="results", bufs=4))
+        results = ctx.enter_context(tc.tile_pool(name="results", bufs=12))
         psum = ctx.enter_context(tc.psum_pool(name="psum", bufs=PSUM_BANKS))
 
         ident = keep.tile([P, P], F32, name="ident")
         x_sb = [keep.tile([P, K], BF16, name="x%d" % m) for m in range(TOKEN_TILES)]
-        cos_sb = [keep.tile([P, N], BF16, name="cos%d" % m) for m in range(TOKEN_TILES)]
-        sin_sb = [keep.tile([P, N], BF16, name="sin%d" % m) for m in range(TOKEN_TILES)]
         grouped = [
             keep.tile([P, K], BF16, name="grouped%d" % m, align_bytes=64)
             for m in range(TOKEN_TILES)
@@ -94,10 +100,26 @@ def tile_attention_pa_kernel(
             keep.tile([P, K // PACK], U8, name="x_scales%d" % m, align_bytes=64)
             for m in range(TOKEN_TILES)
         ]
+        cos_sb = [
+            [keep.tile([P, 2, BANK], BF16, name="cos%d_%d" % (j, m)) for m in range(TOKEN_TILES)]
+            for j in range(PAIRS)
+        ]
+        sin_sb = [
+            [keep.tile([P, 2, BANK], BF16, name="sin%d_%d" % (j, m)) for m in range(TOKEN_TILES)]
+            for j in range(PAIRS)
+        ]
         w_words = [
             [
-                keep.tile([P, 2 * N], U8, name="w_words%d_%d" % (w, g), align_bytes=64)
-                for g in range(K_GROUPS)
+                [
+                    keep.tile(
+                        [P, 2, FP4_WORD_BYTES * BANK],
+                        U8,
+                        name="w_words%d_%d_%d" % (w, j, g),
+                        align_bytes=64,
+                    )
+                    for g in range(K_GROUPS)
+                ]
+                for j in range(PAIRS)
             ]
             for w in range(2)
         ]
@@ -112,11 +134,19 @@ def tile_attention_pa_kernel(
 
         for m in range(TOKEN_TILES):
             nc.sync.dma_start(out=x_sb[m][:], in_=x_rows[m * P : (m + 1) * P, :])
-        load_weight(nc, Wq_words, Wq_scales, w_words[0], w_planes[0])
-        for m in range(TOKEN_TILES):
-            nc.sync.dma_start(out=cos_sb[m][:], in_=cos[m * P : (m + 1) * P, :])
-            nc.sync.dma_start(out=sin_sb[m][:], in_=sin[m * P : (m + 1) * P, :])
-        load_weight(nc, Wk_words, Wk_scales, w_words[1], w_planes[1])
+        for w in range(2):
+            load_scales(nc, scales_dram[w], w_planes[w])
+            for j in range(PAIRS):
+                for g in range(K_GROUPS):
+                    nc.sync.dma_start(
+                        out=w_words[w][j][g][:].bitcast(I32),
+                        in_=pair_columns(words_dram[w][g].bitcast(I32), j),
+                    )
+                if w == 0:
+                    for m in range(TOKEN_TILES):
+                        rows = slice(m * P, (m + 1) * P)
+                        nc.sync.dma_start(out=cos_sb[j][m][:], in_=pair_columns(cos[rows, :], j))
+                        nc.sync.dma_start(out=sin_sb[j][m][:], in_=pair_columns(sin[rows, :], j))
 
         for m in range(TOKEN_TILES):
             transpose_tokens(nc, psum, x_sb[m], ident, grouped[m])
@@ -126,50 +156,45 @@ def tile_attention_pa_kernel(
             )
 
         for w in range(2):
-            for m in range(TOKEN_TILES):
-                rotated = results.tile([P, 2, PAIRS, BANK], F32)
-                for j in range(PAIRS):
-                    low_start = j * BANK
-                    high_start = HALF + j * BANK
-                    low = slice(low_start, low_start + BANK)
-                    high = slice(high_start, high_start + BANK)
-                    acc_low = psum.tile([P, BANK], F32, tag="bank")
-                    acc_high = psum.tile([P, BANK], F32, tag="bank")
+            for j in range(PAIRS):
+                for m in range(TOKEN_TILES):
+                    acc = [psum.tile([P, BANK], F32, tag="bank", name="acc%d" % h) for h in range(2)]
                     for g in range(K_GROUPS):
                         tokens = slice(g * P, (g + 1) * P)
-                        for acc, first in ((acc_low, low_start), (acc_high, high_start)):
+                        for h in (LOW, HIGH):
+                            first = h * HALF + j * BANK
                             nc.tensor.matmul_mx(
-                                out=acc[:],
+                                out=acc[h][:],
                                 lhsT=x_codes[m][:, tokens].bitcast(FP8X4),
                                 lhsT_scale=x_scales[m][:, tokens],
-                                rhs=w_words[w][g][:, 2 * first : 2 * (first + BANK)].bitcast(FP4X4),
+                                rhs=w_words[w][j][g][:, h, :].bitcast(FP4X4),
                                 rhs_scale=w_planes[w][:, g, first : first + BANK],
                                 start=(g == 0),
                                 stop=(g == K_GROUPS - 1),
                             )
+                    cos_jm = cos_sb[j][m]
+                    sin_jm = sin_sb[j][m]
                     by_cos = parts.tile([P, 2, BANK], F32)
                     by_sin = parts.tile([P, 2, BANK], F32)
+                    for h in (LOW, HIGH):
+                        nc.vector.tensor_tensor(
+                            out=by_cos[:, h, :], in0=acc[h][:], in1=cos_jm[:, h, :], op=MULT
+                        )
                     nc.vector.tensor_tensor(
-                        out=by_cos[:, 0, :], in0=acc_low[:], in1=cos_sb[m][:, low], op=MULT
-                    )
-                    nc.vector.tensor_tensor(
-                        out=by_sin[:, 1, :], in0=acc_low[:], in1=sin_sb[m][:, high], op=MULT
-                    )
-                    nc.vector.tensor_tensor(
-                        out=by_cos[:, 1, :], in0=acc_high[:], in1=cos_sb[m][:, high], op=MULT
+                        out=by_sin[:, HIGH, :], in0=acc[LOW][:], in1=sin_jm[:, HIGH, :], op=MULT
                     )
                     nc.vector.scalar_tensor_tensor(
-                        out=by_sin[:, 0, :],
-                        in0=acc_high[:],
+                        out=by_sin[:, LOW, :],
+                        in0=acc[HIGH][:],
                         scalar=-1.0,
-                        in1=sin_sb[m][:, low],
+                        in1=sin_jm[:, LOW, :],
                         op0=MULT,
                         op1=MULT,
                     )
-                    nc.gpsimd.tensor_tensor(
-                        out=rotated[:, :, j, :], in0=by_cos[:], in1=by_sin[:], op=ADD
+                    is_last = w == 1 and j == PAIRS - 1 and m == TOKEN_TILES - 1
+                    adder = nc.vector if is_last else nc.gpsimd
+                    rotated = results.tile([P, 2, BANK], F32)
+                    adder.tensor_tensor(out=rotated[:], in0=by_cos[:], in1=by_sin[:], op=ADD)
+                    nc.sync.dma_start(
+                        out=pair_columns(outs_dram[w][m * P : (m + 1) * P, :], j), in_=rotated[:]
                     )
-                nc.sync.dma_start(
-                    out=outs_dram[w][m * P : (m + 1) * P, :],
-                    in_=rotated[:].rearrange("p h j c -> p (h j c)"),
-                )

@@ -30,6 +30,8 @@ PSUM_BANKS = 8
 WORDS_PER_GROUP = K_PASS // 2
 SCALE_ROWS = K_PASS // 32
 FP4_WORD_BYTES = 2
+UNITS = 2 * PAIRS * TOKEN_TILES
+VECTOR_SUMS = 2
 
 FLOPS = 2 * 2 * TOKENS * K * N
 
@@ -155,6 +157,7 @@ def tile_attention_pa_kernel(
                 out=x_codes[m][:].bitcast(FP8X4), scales=x_scales[m][:], in_=grouped[m][:]
             )
 
+        left_over = []
         for w in range(2):
             for j in range(PAIRS):
                 for m in range(TOKEN_TILES):
@@ -191,10 +194,22 @@ def tile_attention_pa_kernel(
                         op0=MULT,
                         op1=MULT,
                     )
-                    is_last = w == 1 and j == PAIRS - 1 and m == TOKEN_TILES - 1
-                    adder = nc.vector if is_last else nc.gpsimd
                     rotated = results.tile([P, 2, BANK], F32)
-                    adder.tensor_tensor(out=rotated[:], in0=by_cos[:], in1=by_sin[:], op=ADD)
-                    nc.sync.dma_start(
-                        out=pair_columns(outs_dram[w][m * P : (m + 1) * P, :], j), in_=rotated[:]
-                    )
+                    unit = (w * PAIRS + j) * TOKEN_TILES + m
+                    if unit < UNITS - VECTOR_SUMS:
+                        nc.gpsimd.tensor_tensor(out=rotated[:], in0=by_cos[:], in1=by_sin[:], op=ADD)
+                        nc.sync.dma_start(
+                            out=pair_columns(outs_dram[w][m * P : (m + 1) * P, :], j), in_=rotated[:]
+                        )
+                    else:
+                        left_over.append((w, j, m, by_cos, by_sin, rotated))
+
+        for w, j, m, by_cos, by_sin, rotated in left_over:
+            for h in (LOW, HIGH):
+                nc.vector.tensor_tensor(
+                    out=rotated[:, h, :], in0=by_cos[:, h, :], in1=by_sin[:, h, :], op=ADD
+                )
+                first = h * HALF + j * BANK
+                nc.sync.dma_start(
+                    out=outs_dram[w][m * P : (m + 1) * P, first : first + BANK], in_=rotated[:, h, :]
+                )

@@ -32,6 +32,7 @@ SCALE_ROWS = K_PASS // 32
 FP4_WORD_BYTES = 2
 UNITS = 2 * PAIRS * TOKEN_TILES
 VECTOR_SUMS = 2
+WARM_UP_MATMULS = 4
 
 FLOPS = 2 * 2 * TOKENS * K * N
 
@@ -152,6 +153,15 @@ def tile_attention_pa_kernel(
 
         for m in range(TOKEN_TILES):
             transpose_tokens(nc, psum, x_sb[m], ident, grouped[m])
+        unread = psum.tile([P, BANK], F32, tag="bank")
+        for i in range(WARM_UP_MATMULS):
+            nc.tensor.matmul(
+                out=unread[:],
+                lhsT=grouped[0][:, 0:P],
+                rhs=grouped[0][:, 0:BANK],
+                start=True,
+                stop=True,
+            )
         for m in range(TOKEN_TILES):
             nc.vector.quantize_mx(
                 out=x_codes[m][:].bitcast(FP8X4), scales=x_scales[m][:], in_=grouped[m][:]

@@ -103,12 +103,8 @@ def tile_attention_pa_kernel(
             keep.tile([P, K // PACK], U8, name="x_scales%d" % m, align_bytes=64)
             for m in range(TOKEN_TILES)
         ]
-        cos_sb = [
-            [keep.tile([P, 2, BANK], BF16, name="cos%d_%d" % (j, m)) for m in range(TOKEN_TILES)]
-            for j in range(PAIRS)
-        ]
-        sin_sb = [
-            [keep.tile([P, 2, BANK], BF16, name="sin%d_%d" % (j, m)) for m in range(TOKEN_TILES)]
+        tables = [
+            [keep.tile([P, 4, BANK], BF16, name="tables%d_%d" % (j, m)) for m in range(TOKEN_TILES)]
             for j in range(PAIRS)
         ]
         w_words = [
@@ -148,11 +144,14 @@ def tile_attention_pa_kernel(
                 if w == 0:
                     for m in range(TOKEN_TILES):
                         rows = slice(m * P, (m + 1) * P)
-                        nc.sync.dma_start(out=cos_sb[j][m][:], in_=pair_columns(cos[rows, :], j))
-                        nc.sync.dma_start(out=sin_sb[j][m][:], in_=pair_columns(sin[rows, :], j))
+                        nc.sync.dma_start(out=tables[j][m][:, 0:4:2, :], in_=pair_columns(cos[rows, :], j))
+                        nc.sync.dma_start(out=tables[j][m][:, 1:4:2, :], in_=pair_columns(sin[rows, :], j))
 
         for m in range(TOKEN_TILES):
             transpose_tokens(nc, psum, x_sb[m], ident, grouped[m])
+        for j in range(PAIRS):
+            for m in range(TOKEN_TILES):
+                nc.scalar.mul(out=tables[j][m][:, 1, :], in_=tables[j][m][:, 1, :], mul=-1.0)
         unread = psum.tile([P, BANK], F32, tag="bank")
         for i in range(WARM_UP_MATMULS):
             nc.tensor.matmul(
@@ -185,24 +184,19 @@ def tile_attention_pa_kernel(
                                 start=(g == 0),
                                 stop=(g == K_GROUPS - 1),
                             )
-                    cos_jm = cos_sb[j][m]
-                    sin_jm = sin_sb[j][m]
                     by_cos = parts.tile([P, 2, BANK], F32)
                     by_sin = parts.tile([P, 2, BANK], F32)
-                    for h in (LOW, HIGH):
-                        nc.vector.tensor_tensor(
-                            out=by_cos[:, h, :], in0=acc[h][:], in1=cos_jm[:, h, :], op=MULT
-                        )
                     nc.vector.tensor_tensor(
-                        out=by_sin[:, HIGH, :], in0=acc[LOW][:], in1=sin_jm[:, HIGH, :], op=MULT
+                        out=by_cos[:],
+                        in0=acc[LOW][:].unsqueeze(1).to_broadcast([P, 2, BANK]),
+                        in1=tables[j][m][:, 0:4:3, :],
+                        op=MULT,
                     )
-                    nc.vector.scalar_tensor_tensor(
-                        out=by_sin[:, LOW, :],
-                        in0=acc[HIGH][:],
-                        scalar=-1.0,
-                        in1=sin_jm[:, LOW, :],
-                        op0=MULT,
-                        op1=MULT,
+                    nc.vector.tensor_tensor(
+                        out=by_sin[:],
+                        in0=acc[HIGH][:].unsqueeze(1).to_broadcast([P, 2, BANK]),
+                        in1=tables[j][m][:, 1:3, :],
+                        op=MULT,
                     )
                     rotated = results.tile([P, 2, BANK], F32)
                     unit = (w * PAIRS + j) * TOKEN_TILES + m

from contextlib import ExitStack

import concourse.mybir as mybir
from concourse.masks import make_identity

F32 = mybir.dt.float32
BF16 = mybir.dt.bfloat16
I32 = mybir.dt.int32
U32 = mybir.dt.uint32
U8 = mybir.dt.uint8
FP8X4 = mybir.dt.float8_e4m3fn_x4
FP4X4 = mybir.dt.float4_e2m1fn_x4
MULT = mybir.AluOpType.mult
ADD = mybir.AluOpType.add

P = 128
TOKENS = 512
K = 2048
N = 2048
HALF = N // 2
PACK = 4
K_PASS = P * PACK
K_GROUPS = K // K_PASS
TOKEN_TILES = TOKENS // P
BANK = 512
PAIRS = HALF // BANK
LOW = 0
HIGH = 1
PSUM_BANKS = 8
WORDS_PER_GROUP = K_PASS // 2
SCALE_ROWS = K_PASS // 32
FP4_WORD_BYTES = 2
UNITS = 2 * PAIRS * TOKEN_TILES
VECTOR_SUMS = 2
WARM_UP_MATMULS = 4

FLOPS = 2 * 2 * TOKENS * K * N


def pair_columns(rows, j):
    width = rows.shape[1] // (2 * PAIRS)
    return rows.rearrange("r (h c) -> r h c", h=2)[:, :, j * width : (j + 1) * width]


def load_scales(nc, scales_dram, plane):
    for g in range(0, K_GROUPS, 2):
        for s in range(SCALE_ROWS // 2):
            first = 32 * (s // 4) + s % 4
            nc.sync.dma_start(
                out=plane[first : P : P // 2, g : g + 2, :].bitcast(I32),
                in_=scales_dram[g : g + 2, s : SCALE_ROWS : SCALE_ROWS // 2, :]
                .bitcast(I32)
                .rearrange("g s n -> s g n"),
            )


def transpose_tokens(nc, psum, x_tile, ident, grouped):
    x_words = x_tile[:].bitcast(F32)
    grouped_words = grouped[:].bitcast(F32).rearrange("p (g r u) -> p g r u", g=K_GROUPS, u=2)
    for g in range(0, K_GROUPS, 2):
        turned = psum.tile([P, 2, 2, P], F32, tag="bank")
        for i in range(2):
            for u in range(2):
                start = (g + i) * WORDS_PER_GROUP + u
                nc.tensor.transpose(
                    turned[:, i, u, :],
                    x_words[:, start : (g + i + 1) * WORDS_PER_GROUP : 2],
                    ident[:],
                )
        nc.scalar.copy(
            out=grouped_words[:, g : g + 2, :, :],
            in_=turned[:].rearrange("p g u r -> p g r u"),
        )


def tile_attention_pa_kernel(
    tc, x, cos, sin, Wq_words, Wq_scales, Wk_words, Wk_scales, out_0, out_1
):
    nc = tc.nc
    x_rows = x.flatten_outer_dims()
    words_dram = (Wq_words, Wk_words)
    scales_dram = (Wq_scales, Wk_scales)
    outs_dram = (out_0.flatten_outer_dims(), out_1.flatten_outer_dims())

    with ExitStack() as ctx:
        ctx.enter_context(tc.manual_schedule())
        keep = ctx.enter_context(tc.tile_pool(name="keep", bufs=1))
        parts = ctx.enter_context(tc.tile_pool(name="parts", bufs=3))
        results = ctx.enter_context(tc.tile_pool(name="results", bufs=12))
        psum = ctx.enter_context(tc.psum_pool(name="psum", bufs=PSUM_BANKS))

        ident = keep.tile([P, P], F32, name="ident")
        x_sb = [keep.tile([P, K], BF16, name="x%d" % m) for m in range(TOKEN_TILES)]
        grouped = [
            keep.tile([P, K], BF16, name="grouped%d" % m, align_bytes=64)
            for m in range(TOKEN_TILES)
        ]
        x_codes = [
            keep.tile([P, K // PACK], U32, name="x_codes%d" % m, align_bytes=64)
            for m in range(TOKEN_TILES)
        ]
        x_scales = [
            keep.tile([P, K // PACK], U8, name="x_scales%d" % m, align_bytes=64)
            for m in range(TOKEN_TILES)
        ]
        tables = [
            [keep.tile([P, 4, BANK], BF16, name="tables%d_%d" % (j, m)) for m in range(TOKEN_TILES)]
            for j in range(PAIRS)
        ]
        w_words = [
            [
                [
                    keep.tile(
                        [P, 2, FP4_WORD_BYTES * BANK],
                        U8,
                        name="w_words%d_%d_%d" % (w, j, g),
                        align_bytes=64,
                    )
                    for g in range(K_GROUPS)
                ]
                for j in range(PAIRS)
            ]
            for w in range(2)
        ]
        w_planes = [
            keep.tile([P, K_GROUPS, N], U8, name="w_plane%d" % w, align_bytes=64)
            for w in range(2)
        ]

        make_identity(nc, ident[:])
        for w in range(2):
            nc.vector.memset(w_planes[w][:].bitcast(I32), 0)

        for m in range(TOKEN_TILES):
            nc.sync.dma_start(out=x_sb[m][:], in_=x_rows[m * P : (m + 1) * P, :])
        for w in range(2):
            load_scales(nc, scales_dram[w], w_planes[w])
            for j in range(PAIRS):
                for g in range(K_GROUPS):
                    nc.sync.dma_start(
                        out=w_words[w][j][g][:].bitcast(I32),
                        in_=pair_columns(words_dram[w][g].bitcast(I32), j),
                    )
                if w == 0:
                    for m in range(TOKEN_TILES):
                        rows = slice(m * P, (m + 1) * P)
                        nc.sync.dma_start(out=tables[j][m][:, 0:4:2, :], in_=pair_columns(cos[rows, :], j))
                        nc.sync.dma_start(out=tables[j][m][:, 1:4:2, :], in_=pair_columns(sin[rows, :], j))

        for m in range(TOKEN_TILES):
            transpose_tokens(nc, psum, x_sb[m], ident, grouped[m])
        for j in range(PAIRS):
            for m in range(TOKEN_TILES):
                nc.scalar.mul(out=tables[j][m][:, 1, :], in_=tables[j][m][:, 1, :], mul=-1.0)
        unread = psum.tile([P, BANK], F32, tag="bank")
        for i in range(WARM_UP_MATMULS):
            nc.tensor.matmul(
                out=unread[:],
                lhsT=grouped[0][:, 0:P],
                rhs=grouped[0][:, 0:BANK],
                start=True,
                stop=True,
            )
        for m in range(TOKEN_TILES):
            nc.vector.quantize_mx(
                out=x_codes[m][:].bitcast(FP8X4), scales=x_scales[m][:], in_=grouped[m][:]
            )

        left_over = []
        for w in range(2):
            for j in range(PAIRS):
                for m in range(TOKEN_TILES):
                    acc = [psum.tile([P, BANK], F32, tag="bank", name="acc%d" % h) for h in range(2)]
                    for g in range(K_GROUPS):
                        tokens = slice(g * P, (g + 1) * P)
                        for h in (LOW, HIGH):
                            first = h * HALF + j * BANK
                            nc.tensor.matmul_mx(
                                out=acc[h][:],
                                lhsT=x_codes[m][:, tokens].bitcast(FP8X4),
                                lhsT_scale=x_scales[m][:, tokens],
                                rhs=w_words[w][j][g][:, h, :].bitcast(FP4X4),
                                rhs_scale=w_planes[w][:, g, first : first + BANK],
                                start=(g == 0),
                                stop=(g == K_GROUPS - 1),
                            )
                    by_cos = parts.tile([P, 2, BANK], F32)
                    by_sin = parts.tile([P, 2, BANK], F32)
                    nc.vector.tensor_tensor(
                        out=by_cos[:],
                        in0=acc[LOW][:].unsqueeze(1).to_broadcast([P, 2, BANK]),
                        in1=tables[j][m][:, 0:4:3, :],
                        op=MULT,
                    )
                    nc.vector.tensor_tensor(
                        out=by_sin[:],
                        in0=acc[HIGH][:].unsqueeze(1).to_broadcast([P, 2, BANK]),
                        in1=tables[j][m][:, 1:3, :],
                        op=MULT,
                    )
                    rotated = results.tile([P, 2, BANK], F32)
                    unit = (w * PAIRS + j) * TOKEN_TILES + m
                    if unit < UNITS - VECTOR_SUMS:
                        nc.gpsimd.tensor_tensor(out=rotated[:], in0=by_cos[:], in1=by_sin[:], op=ADD)
                        nc.sync.dma_start(
                            out=pair_columns(outs_dram[w][m * P : (m + 1) * P, :], j), in_=rotated[:]
                        )
                    else:
                        left_over.append((w, j, m, by_cos, by_sin, rotated))

        for w, j, m, by_cos, by_sin, rotated in left_over:
            for h in (LOW, HIGH):
                nc.vector.tensor_tensor(
                    out=rotated[:, h, :], in0=by_cos[:, h, :], in1=by_sin[:, h, :], op=ADD
                )
                first = h * HALF + j * BANK
                nc.sync.dma_start(
                    out=outs_dram[w][m * P : (m + 1) * P, first : first + BANK], in_=rotated[:, h, :]
                )
